import numpy as np
import ml_dtypes


def mxq(x, axis, fmt="e4m3"):
    dtype, down = {"e4m3": (ml_dtypes.float8_e4m3fn, 7), "e5m2": (ml_dtypes.float8_e5m2, 14)}[fmt]
    v = np.moveaxis(np.asarray(x, np.float32).astype(ml_dtypes.bfloat16).astype(np.float64), axis, -1)
    blocks = v.reshape(v.shape[:-1] + (-1, 32))
    amax = np.abs(blocks).max(-1, keepdims=True)
    byte = np.maximum(np.where(amax > 0, np.frexp(amax)[1] - 1 + 127, 0) - down, 1)
    scale = np.exp2(byte - 127.0)
    codes = (blocks / scale).astype(np.float32).astype(dtype).astype(np.float64)
    return np.moveaxis((codes * scale).reshape(v.shape), -1, axis)


WIDE = False


def mx_kscale(k):
    if not WIDE:
        return np.ones(k)
    levels = np.array([10, -10, 5, -5, 0])
    if k % 512:
        return np.exp2(np.random.permutation(np.resize(levels, k // 32))).repeat(32)
    a = np.empty((k // 512, 16))
    for p in range(k // 512):
        a[p, :8] = np.random.permutation(np.resize(levels, 8))
        for g in range(8):
            far = levels[np.abs(levels - a[p, g]) >= 10]
            a[p, g + 8] = far[np.random.randint(len(far))]
    return np.exp2(a.ravel()).repeat(32)


BF16 = ml_dtypes.bfloat16


def bf(x):
    return np.asarray(x, np.float32).astype(BF16)


def f64(x):
    return np.asarray(x).astype(np.float64)


B, S, D, H, F = 2, 2048, 512, 8, 2816
DK = D // H
EPS = 1e-5
ROPE_THETA = 10000.0


def rmsnorm(x, gains):
    rms = np.sqrt(np.mean(np.square(x), axis=-1, keepdims=True) + EPS)
    return (x * gains) / rms


def rope_tables():
    inv = ROPE_THETA ** (-(2.0 * np.arange(DK // 2)) / DK)
    ang = np.arange(S)[:, None] * inv[None, :]
    ang = np.repeat(ang, 2, axis=-1)
    return np.cos(ang), np.sin(ang)


def apply_rope(t, cos, sin):
    tr = t.reshape(*t.shape[:-1], -1, 2)
    t_flip = np.stack([-tr[..., 1], tr[..., 0]], axis=-1).reshape(t.shape)
    return t * cos + t_flip * sin


def heads(p):
    return p.reshape(B, S, H, DK).transpose(0, 2, 1, 3)


def setup_inputs():
    s = mx_kscale(D)
    tok = np.where(np.random.random((B, S, 1)) < 0.25, 0.004, 1.0)
    return {"x": bf(np.random.standard_normal((B, S, D)) * tok),
            "gains1": bf((1.0 + 0.25 * np.random.standard_normal(D)) * s),
            "WQ": bf(np.random.standard_normal((D, D)) / np.sqrt(D) / s[None, :]),
            "WK": bf(np.random.standard_normal((D, D)) / np.sqrt(D) / s[None, :]),
            "WV": bf(np.random.standard_normal((D, D)) / np.sqrt(D) / s[None, :])}


def reference(x, gains1, WQ, WK, WV):
    h = mxq(rmsnorm(f64(x), f64(gains1)), 2, "e4m3")
    q = heads(h @ mxq(f64(WQ), 1, "e4m3").T)
    k = heads(h @ mxq(f64(WK), 1, "e4m3").T)
    v = heads(h @ mxq(f64(WV), 1, "e4m3").T)
    cos, sin = rope_tables()
    return apply_rope(q, cos, sin), apply_rope(k, cos, sin), v

@@ -1,0 +1,307 @@
+import math
+from contextlib import ExitStack
+
+import concourse.mybir as mybir
+from concourse.masks import make_identity
+
+F32 = mybir.dt.float32
+BF16 = mybir.dt.bfloat16
+I32 = mybir.dt.int32
+U32 = mybir.dt.uint32
+U8 = mybir.dt.uint8
+FP8X4 = mybir.dt.float8_e4m3fn_x4
+ALU = mybir.AluOpType
+ACT = mybir.ActivationFunctionType
+
+P = 128
+BATCH, SEQ, FEAT, HEADS, HEAD_DIM = 2, 2048, 512, 8, 64
+PAIRS = HEAD_DIM // 2
+HALF = FEAT // 2
+EPS = 1e-5
+ROPE_THETA = 10000.0
+PACK = 4
+RUN = 4
+GROUP = P * RUN
+GROUPS = BATCH * SEQ // GROUP
+GROUPS_PER_BATCH = SEQ // GROUP
+SLOTS = SEQ // P
+TILES = GROUPS * RUN
+STEP = 2
+STEPS = TILES // STEP
+STEPS_PER_GROUP = RUN // STEP
+AHEAD = 2
+ROUND_MAGIC = 1.5 * 2.0**23
+
+FLOPS = 2 * BATCH * SEQ * FEAT * 3 * FEAT
+
+
+def tile_prenormtransformer_pa_t_kernel(tc, x, gains1, WQ, WK, WV, out_0, out_1, out_2):
+    nc = tc.nc
+    tokens = x.flatten_outer_dims()
+
+    with ExitStack() as ctx:
+        const = ctx.enter_context(tc.tile_pool(name="const", bufs=1))
+        setup = ctx.enter_context(tc.tile_pool(name="setup", bufs=1))
+        wload = ctx.enter_context(tc.tile_pool(name="wload", bufs=2))
+        small = ctx.enter_context(tc.tile_pool(name="small", bufs=3))
+        norm = ctx.enter_context(tc.tile_pool(name="norm", bufs=4))
+        packed = ctx.enter_context(tc.tile_pool(name="packed", bufs=AHEAD + 2))
+        rope = ctx.enter_context(tc.tile_pool(name="rope", bufs=3))
+        stage = ctx.enter_context(tc.tile_pool(name="stage", bufs=3))
+        psum_turn = ctx.enter_context(tc.psum_pool(name="turn", bufs=2))
+        psum_acc = ctx.enter_context(tc.psum_pool(name="acc", bufs=6))
+
+        x_all = const.tile([P, GROUPS, RUN * FEAT], BF16)
+
+        def load_group(g):
+            nc.sync.dma_start(
+                out=x_all[:, g, :],
+                in_=tokens[g * GROUP : (g + 1) * GROUP, :].rearrange("(p i) k -> p (i k)", i=RUN),
+            )
+
+        load_group(0)
+        raw = {}
+        for name, w in (("q", WQ), ("k", WK)):
+            w_raw = const.tile([P, PACK * FEAT], BF16, name="raw_" + name)
+            nc.sync.dma_start(
+                out=w_raw[:].rearrange("p (c r) -> p c r", c=2),
+                in_=w.rearrange("(c p e) k -> p c (e k)", p=P, e=2),
+            )
+            raw[name] = w_raw
+        v_raw = const.tile([P, PACK * FEAT], BF16)
+        nc.sync.dma_start(
+            out=v_raw[:].rearrange("p (c k) -> p c k", c=PACK),
+            in_=WV.rearrange("(c p) k -> p c k", p=P),
+        )
+        raw["v"] = v_raw
+        for g in range(1, GROUPS):
+            load_group(g)
+
+        gain_rows = setup.tile([P, FEAT], BF16)
+        nc.vector.memset(gain_rows[:], 0.0)
+        nc.scalar.dma_start(out=gain_rows[0:1, :], in_=gains1.unsqueeze(0))
+
+        pos_int = setup.tile([P, SLOTS], I32)
+        nc.gpsimd.iota(
+            pos_int[:], pattern=[[GROUP, GROUPS_PER_BATCH], [1, RUN]], base=0, channel_multiplier=RUN
+        )
+        ident = const.tile([P, P], F32)
+        make_identity(nc, ident[:])
+        pos = setup.tile([P, SLOTS], F32)
+        nc.vector.tensor_copy(out=pos[:], in_=pos_int[:])
+        turns = setup.tile([P, 2, SLOTS, PAIRS], F32)
+        for j in range(PAIRS):
+            nc.vector.tensor_scalar(
+                out=turns[:, 0, :, j],
+                in0=pos[:],
+                scalar1=ROPE_THETA ** (-2.0 * j / HEAD_DIM) / (2.0 * math.pi),
+                scalar2=None,
+                op0=ALU.mult,
+            )
+        nc.vector.tensor_scalar(
+            out=turns[:, 1], in0=turns[:, 0], scalar1=0.25, scalar2=None, op0=ALU.add
+        )
+        whole = setup.tile([P, 2, SLOTS, PAIRS], F32)
+        nc.vector.tensor_scalar(
+            out=whole[:], in0=turns[:], scalar1=ROUND_MAGIC, scalar2=ROUND_MAGIC,
+            op0=ALU.add, op1=ALU.subtract,
+        )
+        part = setup.tile([P, 2, SLOTS, PAIRS], F32)
+        nc.vector.tensor_tensor(out=part[:], in0=turns[:], in1=whole[:], op=ALU.subtract)
+        sin_cos = const.tile([P, 2, SLOTS, PAIRS], F32)
+        nc.scalar.activation(out=sin_cos[:], in_=part[:], func=ACT.Sin, scale=2.0 * math.pi)
+        sin_tab = sin_cos[:, 0]
+        cos_tab = sin_cos[:, 1]
+        mix_tab = const.tile([P, SLOTS, PAIRS, 2], F32)
+        nc.vector.scalar_tensor_tensor(
+            out=mix_tab[:, :, :, 0], in0=cos_tab, scalar=-1.0, in1=sin_tab,
+            op0=ALU.mult, op1=ALU.subtract,
+        )
+        nc.vector.tensor_tensor(out=mix_tab[:, :, :, 1], in0=sin_tab, in1=cos_tab, op=ALU.subtract)
+
+        gain_bank = psum_acc.tile([P, FEAT], F32, tag="acc")
+        for u in range(2):
+            nc.tensor.transpose(
+                gain_bank[:, u * P : (u + 1) * P], gain_rows[:].bitcast(F32)[:, u:HALF:2], ident[:]
+            )
+        gain_words = const.tile([P, 2], F32)
+        nc.vector.tensor_copy(out=gain_words[:], in_=gain_bank[:, 0 : 2 * P : P])
+        gain_col = gain_words[:].bitcast(BF16)
+
+        rstd_of = {}
+
+        def group_stats(g):
+            squares = norm.tile([P, RUN * FEAT], BF16, tag="squares", bufs=2)
+            sumsq = small.tile([P, RUN], F32)
+            for i in range(RUN):
+                cols = slice(i * FEAT, (i + 1) * FEAT)
+                nc.scalar.activation(
+                    out=squares[:, cols], in_=x_all[:, g, cols], func=ACT.Square,
+                    accum_out=sumsq[:, i : i + 1],
+                )
+            meansq = small.tile([P, RUN], F32)
+            nc.vector.tensor_scalar(
+                out=meansq[:], in0=sumsq[:], scalar1=1.0 / FEAT, scalar2=EPS,
+                op0=ALU.mult, op1=ALU.add,
+            )
+            rms = small.tile([P, RUN], F32)
+            nc.scalar.activation(out=rms[:], in_=meansq[:], func=ACT.Sqrt)
+            rstd = small.tile([P, RUN], F32)
+            nc.vector.reciprocal(out=rstd[:], in_=rms[:])
+            rstd_of[g] = rstd
+
+        group_stats(0)
+
+        w_codes = {}
+        w_scales = {}
+        for name in ("q", "k", "v"):
+            words = raw[name][:].bitcast(F32)
+            w_grouped = wload.tile([P, FEAT * PACK], BF16, align_bytes=64)
+            grouped_words = w_grouped[:].bitcast(F32)
+            for half in range(2):
+                bank = psum_acc.tile([P, FEAT], F32, tag="acc")
+                for inner in range(2):
+                    block = 2 * half + inner
+                    chunk = block if name == "v" else 2 * (block % 2) + 1 - block // 2
+                    for u in range(2):
+                        nc.tensor.transpose(
+                            bank[:, (2 * inner + u) * P : (2 * inner + u + 1) * P],
+                            words[:, chunk * HALF + u : (chunk + 1) * HALF : 2],
+                            ident[:],
+                        )
+                dst = grouped_words[:, half * FEAT : (half + 1) * FEAT].rearrange(
+                    "p (b r u) -> p b r u", b=2, u=2
+                )
+                src = bank[:].rearrange("p (b u r) -> p b r u", b=2, u=2)
+                if half == 0:
+                    nc.vector.tensor_copy(out=dst, in_=src)
+                else:
+                    nc.scalar.copy(out=dst, in_=src)
+            codes = const.tile([P, FEAT], U32, name="codes_" + name, align_bytes=64)
+            scales = const.tile([P, FEAT], U8, name="scales_" + name, align_bytes=64)
+            nc.vector.quantize_mx(out=codes[:].bitcast(FP8X4), scales=scales[:], in_=w_grouped[:])
+            w_codes[name] = codes
+            w_scales[name] = scales
+
+        def quantise_step(step):
+            g = step // STEPS_PER_GROUP
+            h_grouped = norm.tile([P, STEP, P, PACK], BF16, align_bytes=64)
+            for inner in range(STEP):
+                i = (step % STEPS_PER_GROUP) * STEP + inner
+                scaled = norm.tile([P, FEAT], F32)
+                nc.scalar.activation(
+                    out=scaled[:].rearrange("p (t q) -> p t q", t=PACK),
+                    in_=x_all[:, g, i * FEAT : (i + 1) * FEAT].rearrange("p (q t) -> p t q", t=PACK),
+                    func=ACT.Copy,
+                    scale=rstd_of[g][:, i : i + 1],
+                )
+                turned = psum_turn.tile([P, FEAT], F32)
+                for t in range(PACK):
+                    nc.tensor.transpose(
+                        turned[:, t * P : (t + 1) * P], scaled[:, t * P : (t + 1) * P], ident[:]
+                    )
+                nc.vector.tensor_tensor(
+                    out=h_grouped[:, inner],
+                    in0=turned[:].rearrange("p (t r) -> p r t", t=PACK),
+                    in1=gain_col.unsqueeze(1).to_broadcast([P, P, PACK]),
+                    op=ALU.mult,
+                )
+            h_codes = packed.tile([P, STEP * P], U32, align_bytes=64)
+            h_scales = packed.tile([P, STEP * P], U8, align_bytes=64)
+            nc.vector.quantize_mx(
+                out=h_codes[:].bitcast(FP8X4),
+                scales=h_scales[:],
+                in_=h_grouped[:].rearrange("p a r t -> p (a r t)"),
+            )
+            return h_codes, h_scales
+
+        def mx_pass(out, lhs, name, cols, start, stop):
+            nc.tensor.matmul_mx(
+                out=out,
+                lhsT=lhs[0].bitcast(FP8X4),
+                lhsT_scale=lhs[1],
+                rhs=w_codes[name][:, cols].bitcast(FP8X4),
+                rhs_scale=w_scales[name][:, cols],
+                start=start,
+                stop=stop,
+            )
+
+        def project_tile(lhs, slot, i, stage_qk, stage_v):
+            everything = slice(0, FEAT)
+            odd_rows = slice(0, HALF)
+            even_rows = slice(HALF, FEAT)
+            swapped = {}
+            for name in ("q", "k"):
+                bank = psum_acc.tile([P, FEAT], F32, tag="acc", name="swapped_" + name)
+                mx_pass(bank[:], lhs, name, everything, True, True)
+                swapped[name] = bank
+            sums = psum_acc.tile([P, FEAT], F32, tag="acc")
+            for w, name in enumerate(("q", "k")):
+                mx_pass(sums[:, w * HALF : (w + 1) * HALF], lhs, name, odd_rows, True, False)
+                mx_pass(sums[:, w * HALF : (w + 1) * HALF], lhs, name, even_rows, False, True)
+            values = psum_acc.tile([P, FEAT], F32, tag="acc")
+            mx_pass(values[:], lhs, "v", everything, True, True)
+
+            mixed = rope.tile([P, 2 * HEADS, PAIRS, 2], F32)
+            for w, name in enumerate(("q", "k")):
+                nc.vector.tensor_tensor(
+                    out=mixed[:, w * HEADS : (w + 1) * HEADS],
+                    in0=swapped[name][:].rearrange("p (e h j) -> p h j e", e=2, h=HEADS),
+                    in1=mix_tab[:, slot].unsqueeze(1).to_broadcast([P, HEADS, PAIRS, 2]),
+                    op=ALU.mult,
+                )
+            shared = rope.tile([P, 2 * HEADS, PAIRS], F32)
+            nc.vector.tensor_tensor(
+                out=shared[:],
+                in0=sums[:].rearrange("p (a j) -> p a j", j=PAIRS),
+                in1=cos_tab[:, slot].unsqueeze(1).to_broadcast([P, 2 * HEADS, PAIRS]),
+                op=ALU.mult,
+            )
+            nc.gpsimd.tensor_tensor(
+                out=stage_qk[:, :, i, :].rearrange("p a (j e) -> p a j e", e=2),
+                in0=mixed[:],
+                in1=shared[:].unsqueeze(3).to_broadcast([P, 2 * HEADS, PAIRS, 2]),
+                op=ALU.add,
+            )
+            nc.scalar.copy(
+                out=stage_v[:, :, i, :], in_=values[:].rearrange("p (h d) -> p h d", h=HEADS)
+            )
+
+        def store(dst, b, first, src):
+            nc.sync.dma_start(
+                out=dst[b, :, first : first + GROUP, :].rearrange("h (p i) d -> p h (i d)", i=RUN),
+                in_=src.rearrange("p h i d -> p h (i d)"),
+            )
+
+        ready = {}
+
+        def prepare(step):
+            ready[step] = quantise_step(step)
+            g = step // STEPS_PER_GROUP
+            if step % STEPS_PER_GROUP == 0 and g + 1 < GROUPS:
+                group_stats(g + 1)
+
+        for step in range(AHEAD):
+            prepare(step)
+        stages = {}
+        for step in range(STEPS):
+            g = step // STEPS_PER_GROUP
+            if step + AHEAD < STEPS:
+                prepare(step + AHEAD)
+            if step % STEPS_PER_GROUP == 0:
+                stage_qk = stage.tile([P, 2 * HEADS, RUN, HEAD_DIM], F32)
+                stage_v = stage.tile([P, HEADS, RUN, HEAD_DIM], F32)
+                stages[g] = (stage_qk, stage_v)
+            stage_qk, stage_v = stages[g]
+            h_codes, h_scales = ready[step]
+            for inner in range(STEP):
+                i = (step % STEPS_PER_GROUP) * STEP + inner
+                cols = slice(inner * P, (inner + 1) * P)
+                slot = (g % GROUPS_PER_BATCH) * RUN + i
+                project_tile((h_codes[:, cols], h_scales[:, cols]), slot, i, stage_qk, stage_v)
+            if (step + 1) % STEPS_PER_GROUP == 0:
+                b = g // GROUPS_PER_BATCH
+                first = (g % GROUPS_PER_BATCH) * GROUP
+                store(out_2, b, first, stage_v[:])
+                store(out_0, b, first, stage_qk[:, 0:HEADS])
+                store(out_1, b, first, stage_qk[:, HEADS : 2 * HEADS])

@@ -20,15 +20,14 @@ HALF = FEAT // 2
 EPS = 1e-5
 ROPE_THETA = 10000.0
 PACK = 4
-RUN = 4
-GROUP = P * RUN
-GROUPS = BATCH * SEQ // GROUP
-GROUPS_PER_BATCH = SEQ // GROUP
-SLOTS = SEQ // P
-TILES = GROUPS * RUN
-STEP = 2
-STEPS = TILES // STEP
-STEPS_PER_GROUP = RUN // STEP
+RUNS = (4, 4, 4, 4)
+SLOTS = sum(RUNS)
+QK = 2 * HEADS
+LANES = BATCH * QK
+QUARTERS = 4
+PER_QUARTER = PAIRS // QUARTERS
+QCOLS = QK * PER_QUARTER * 2
+VECTOR_QUARTERS = (3,)
 AHEAD = 2
 ROUND_MAGIC = 1.5 * 2.0**23
 
@@ -37,7 +36,6 @@ FLOPS = 2 * BATCH * SEQ * FEAT * 3 * FEAT
 
 def tile_prenormtransformer_pa_t_kernel(tc, x, gains1, WQ, WK, WV, out_0, out_1, out_2):
     nc = tc.nc
-    tokens = x.flatten_outer_dims()
 
     with ExitStack() as ctx:
         const = ctx.enter_context(tc.tile_pool(name="const", bufs=1))
@@ -46,47 +44,60 @@ def tile_prenormtransformer_pa_t_kernel(tc, x, gains1, WQ, WK, WV, out_0, out_1,
         small = ctx.enter_context(tc.tile_pool(name="small", bufs=3))
         norm = ctx.enter_context(tc.tile_pool(name="norm", bufs=4))
         packed = ctx.enter_context(tc.tile_pool(name="packed", bufs=AHEAD + 2))
-        rope = ctx.enter_context(tc.tile_pool(name="rope", bufs=3))
-        stage = ctx.enter_context(tc.tile_pool(name="stage", bufs=3))
-        psum_turn = ctx.enter_context(tc.psum_pool(name="turn", bufs=2))
-        psum_acc = ctx.enter_context(tc.psum_pool(name="acc", bufs=6))
+        rope = ctx.enter_context(tc.tile_pool(name="rope", bufs=2))
+        stage = ctx.enter_context(tc.tile_pool(name="stage", bufs=2))
+        psum = ctx.enter_context(tc.psum_pool(name="psum", bufs=2))
 
-        x_all = const.tile([P, GROUPS, RUN * FEAT], BF16)
+        firsts = [P * sum(RUNS[:s]) for s in range(len(RUNS))]
+        x_spans = []
 
-        def load_group(g):
-            nc.sync.dma_start(
-                out=x_all[:, g, :],
-                in_=tokens[g * GROUP : (g + 1) * GROUP, :].rearrange("(p i) k -> p (i k)", i=RUN),
-            )
-
-        load_group(0)
-        raw = {}
-        for name, w in (("q", WQ), ("k", WK)):
-            w_raw = const.tile([P, PACK * FEAT], BF16, name="raw_" + name)
-            nc.sync.dma_start(
-                out=w_raw[:].rearrange("p (c r) -> p c r", c=2),
-                in_=w.rearrange("(c p e) k -> p c (e k)", p=P, e=2),
-            )
-            raw[name] = w_raw
-        v_raw = const.tile([P, PACK * FEAT], BF16)
-        nc.sync.dma_start(
-            out=v_raw[:].rearrange("p (c k) -> p c k", c=PACK),
-            in_=WV.rearrange("(c p) k -> p c k", p=P),
-        )
-        raw["v"] = v_raw
-        for g in range(1, GROUPS):
-            load_group(g)
+        def load_span(s):
+            run = RUNS[s]
+            x_span = const.tile([P, BATCH, run * FEAT], BF16, name="x_span%d" % s)
+            for b in range(BATCH):
+                nc.sync.dma_start(
+                    out=x_span[:, b, :],
+                    in_=x[b, firsts[s] : firsts[s] + P * run, :].rearrange("(p i) k -> p (i k)", i=run),
+                )
+            x_spans.append(x_span)
 
         gain_rows = setup.tile([P, FEAT], BF16)
         nc.vector.memset(gain_rows[:], 0.0)
         nc.scalar.dma_start(out=gain_rows[0:1, :], in_=gains1.unsqueeze(0))
+        load_span(0)
+        raw = {}
+        for name, w in (("q", WQ), ("k", WK)):
+            w_raw = const.tile([P, QUARTERS, FEAT], BF16, name="raw_" + name)
+            view = w.rearrange("(m c e) k -> e m c k", c=QUARTERS, e=2)
+            for e in range(2):
+                nc.sync.dma_start(out=w_raw[e:P:2], in_=view[e])
+            raw[name] = w_raw
+        v_raw = const.tile([P, PACK, FEAT], BF16)
+        nc.sync.dma_start(out=v_raw[:], in_=WV.rearrange("(c p) k -> p c k", p=P))
+        for s in range(1, len(RUNS)):
+            load_span(s)
 
-        pos_int = setup.tile([P, SLOTS], I32)
-        nc.gpsimd.iota(
-            pos_int[:], pattern=[[GROUP, GROUPS_PER_BATCH], [1, RUN]], base=0, channel_multiplier=RUN
-        )
         ident = const.tile([P, P], F32)
         make_identity(nc, ident[:])
+        swap = const.tile([P, P], F32)
+        nc.vector.tensor_copy(out=swap[:, 0:P:2], in_=ident[:, 1:P:2])
+        nc.vector.tensor_copy(out=swap[:, 1:P:2], in_=ident[:, 0:P:2])
+        part_int = setup.tile([P, 1], I32)
+        nc.gpsimd.iota(part_int[:], pattern=[[0, 1]], base=0, channel_multiplier=1)
+        odd_int = setup.tile([P, 1], I32)
+        nc.vector.tensor_scalar(out=odd_int[:], in0=part_int[:], scalar1=1, scalar2=None, op0=ALU.bitwise_and)
+        sign = setup.tile([P, 1], F32)
+        nc.vector.tensor_scalar(
+            out=sign[:], in0=odd_int[:], scalar1=-2.0, scalar2=1.0, op0=ALU.mult, op1=ALU.add
+        )
+
+        pos_int = setup.tile([P, SLOTS], I32)
+        slot0 = 0
+        for s, run in enumerate(RUNS):
+            nc.gpsimd.iota(
+                pos_int[:, slot0 : slot0 + run], pattern=[[1, run]], base=firsts[s], channel_multiplier=run
+            )
+            slot0 += run
         pos = setup.tile([P, SLOTS], F32)
         nc.vector.tensor_copy(out=pos[:], in_=pos_int[:])
         turns = setup.tile([P, 2, SLOTS, PAIRS], F32)
@@ -112,14 +123,8 @@ def tile_prenormtransformer_pa_t_kernel(tc, x, gains1, WQ, WK, WV, out_0, out_1,
         nc.scalar.activation(out=sin_cos[:], in_=part[:], func=ACT.Sin, scale=2.0 * math.pi)
         sin_tab = sin_cos[:, 0]
         cos_tab = sin_cos[:, 1]
-        mix_tab = const.tile([P, SLOTS, PAIRS, 2], F32)
-        nc.vector.scalar_tensor_tensor(
-            out=mix_tab[:, :, :, 0], in0=cos_tab, scalar=-1.0, in1=sin_tab,
-            op0=ALU.mult, op1=ALU.subtract,
-        )
-        nc.vector.tensor_tensor(out=mix_tab[:, :, :, 1], in0=sin_tab, in1=cos_tab, op=ALU.subtract)
 
-        gain_bank = psum_acc.tile([P, FEAT], F32, tag="acc")
+        gain_bank = psum.tile([P, FEAT], F32, tag="val")
         for u in range(2):
             nc.tensor.transpose(
                 gain_bank[:, u * P : (u + 1) * P], gain_rows[:].bitcast(F32)[:, u:HALF:2], ident[:]
@@ -130,84 +135,102 @@ def tile_prenormtransformer_pa_t_kernel(tc, x, gains1, WQ, WK, WV, out_0, out_1,
 
         rstd_of = {}
 
-        def group_stats(g):
-            squares = norm.tile([P, RUN * FEAT], BF16, tag="squares", bufs=2)
-            sumsq = small.tile([P, RUN], F32)
-            for i in range(RUN):
-                cols = slice(i * FEAT, (i + 1) * FEAT)
-                nc.scalar.activation(
-                    out=squares[:, cols], in_=x_all[:, g, cols], func=ACT.Square,
-                    accum_out=sumsq[:, i : i + 1],
-                )
-            meansq = small.tile([P, RUN], F32)
+        def span_stats(s):
+            n = BATCH * RUNS[s]
+            squares = norm.tile([P, FEAT], BF16, tag="squares", bufs=2)
+            sumsq = small.tile([P, n], F32)
+            for b in range(BATCH):
+                for i in range(RUNS[s]):
+                    nc.scalar.activation(
+                        out=squares[:], in_=x_spans[s][:, b, i * FEAT : (i + 1) * FEAT], func=ACT.Square,
+                        accum_out=sumsq[:, b * RUNS[s] + i : b * RUNS[s] + i + 1],
+                    )
+            meansq = small.tile([P, n], F32)
             nc.vector.tensor_scalar(
-                out=meansq[:], in0=sumsq[:], scalar1=1.0 / FEAT, scalar2=EPS,
-                op0=ALU.mult, op1=ALU.add,
+                out=meansq[:], in0=sumsq[:], scalar1=1.0 / FEAT, scalar2=EPS, op0=ALU.mult, op1=ALU.add
             )
-            rms = small.tile([P, RUN], F32)
+            rms = small.tile([P, n], F32)
             nc.scalar.activation(out=rms[:], in_=meansq[:], func=ACT.Sqrt)
-            rstd = small.tile([P, RUN], F32)
+            rstd = small.tile([P, n], F32)
             nc.vector.reciprocal(out=rstd[:], in_=rms[:])
-            rstd_of[g] = rstd
+            rstd_of[s] = rstd
 
-        group_stats(0)
+        span_stats(0)
 
-        w_codes = {}
-        w_scales = {}
-        for name in ("q", "k", "v"):
-            words = raw[name][:].bitcast(F32)
-            w_grouped = wload.tile([P, FEAT * PACK], BF16, align_bytes=64)
-            grouped_words = w_grouped[:].bitcast(F32)
-            for half in range(2):
-                bank = psum_acc.tile([P, FEAT], F32, tag="acc")
-                for inner in range(2):
-                    block = 2 * half + inner
-                    chunk = block if name == "v" else 2 * (block % 2) + 1 - block // 2
-                    for u in range(2):
-                        nc.tensor.transpose(
-                            bank[:, (2 * inner + u) * P : (2 * inner + u + 1) * P],
-                            words[:, chunk * HALF + u : (chunk + 1) * HALF : 2],
-                            ident[:],
-                        )
-                dst = grouped_words[:, half * FEAT : (half + 1) * FEAT].rearrange(
-                    "p (b r u) -> p b r u", b=2, u=2
+        turns_of_copies = [0]
+
+        def copy_out(out, in_):
+            if turns_of_copies[0] % 2 == 0:
+                nc.vector.tensor_copy(out=out, in_=in_)
+            else:
+                nc.scalar.copy(out=out, in_=in_)
+            turns_of_copies[0] += 1
+
+        def prepare_columns(codes, scales, cols, w_grouped, chunks, matrix, tag):
+            bank = psum.tile([P, FEAT], F32, tag=tag, name="w_bank")
+            for n, chunk in enumerate(chunks):
+                for u in range(2):
+                    nc.tensor.transpose(
+                        bank[:, (2 * n + u) * P : (2 * n + u + 1) * P], chunk[:, u:HALF:2], matrix[:]
+                    )
+            copy_out(
+                w_grouped[:].bitcast(F32).rearrange("p (b r u) -> p b r u", b=2, u=2),
+                bank[:].rearrange("p (b u r) -> p b r u", b=2, u=2),
+            )
+            nc.vector.quantize_mx(out=codes[:, cols].bitcast(FP8X4), scales=scales[:, cols], in_=w_grouped[:])
+
+        codes_of = {}
+        scales_of = {}
+        for name, width in (("straight", QUARTERS * QCOLS), ("crossed", QUARTERS * QCOLS), ("v", FEAT)):
+            codes_of[name] = const.tile([P, width], U32, name="codes_" + name, align_bytes=64)
+            scales_of[name] = const.tile([P, width], U8, name="scales_" + name, align_bytes=64)
+        signed = {}
+        for name in ("q", "k"):
+            w_signed = const.tile([P, QUARTERS, FEAT], BF16, name="signed_" + name)
+            nc.vector.tensor_scalar(
+                out=w_signed[:], in0=raw[name][:], scalar1=sign[:], scalar2=None, op0=ALU.mult
+            )
+            signed[name] = w_signed
+        for c in range(QUARTERS):
+            cols = slice(c * QCOLS, (c + 1) * QCOLS)
+            for name, source, matrix, tag in (
+                ("straight", raw, ident, "raw"), ("crossed", signed, swap, "rot")
+            ):
+                w_grouped = wload.tile([P, QCOLS * PACK], BF16, align_bytes=64)
+                prepare_columns(
+                    codes_of[name], scales_of[name], cols, w_grouped,
+                    [source[w][:, c, :].bitcast(F32) for w in ("q", "k")], matrix, tag,
                 )
-                src = bank[:].rearrange("p (b u r) -> p b r u", b=2, u=2)
-                if half == 0:
-                    nc.vector.tensor_copy(out=dst, in_=src)
-                else:
-                    nc.scalar.copy(out=dst, in_=src)
-            codes = const.tile([P, FEAT], U32, name="codes_" + name, align_bytes=64)
-            scales = const.tile([P, FEAT], U8, name="scales_" + name, align_bytes=64)
-            nc.vector.quantize_mx(out=codes[:].bitcast(FP8X4), scales=scales[:], in_=w_grouped[:])
-            w_codes[name] = codes
-            w_scales[name] = scales
+        for c in range(2):
+            w_grouped = wload.tile([P, QCOLS * PACK], BF16, align_bytes=64)
+            prepare_columns(
+                codes_of["v"], scales_of["v"], slice(c * QCOLS, (c + 1) * QCOLS), w_grouped,
+                [v_raw[:, 2 * c + n, :].bitcast(F32) for n in range(2)], ident, "val",
+            )
 
-        def quantise_step(step):
-            g = step // STEPS_PER_GROUP
-            h_grouped = norm.tile([P, STEP, P, PACK], BF16, align_bytes=64)
-            for inner in range(STEP):
-                i = (step % STEPS_PER_GROUP) * STEP + inner
+        def quantise_slot(s, i):
+            h_grouped = norm.tile([P, BATCH, P, PACK], BF16, align_bytes=64)
+            for b in range(BATCH):
                 scaled = norm.tile([P, FEAT], F32)
-                nc.scalar.activation(
+                col = b * RUNS[s] + i
+                nc.gpsimd.tensor_scalar(
                     out=scaled[:].rearrange("p (t q) -> p t q", t=PACK),
-                    in_=x_all[:, g, i * FEAT : (i + 1) * FEAT].rearrange("p (q t) -> p t q", t=PACK),
-                    func=ACT.Copy,
-                    scale=rstd_of[g][:, i : i + 1],
+                    in0=x_spans[s][:, b, i * FEAT : (i + 1) * FEAT].rearrange("p (q t) -> p t q", t=PACK),
+                    scalar1=rstd_of[s][:, col : col + 1], scalar2=0.0, op0=ALU.mult, op1=ALU.add,
                 )
-                turned = psum_turn.tile([P, FEAT], F32)
+                turned = psum.tile([P, FEAT], F32, tag="turn")
                 for t in range(PACK):
                     nc.tensor.transpose(
                         turned[:, t * P : (t + 1) * P], scaled[:, t * P : (t + 1) * P], ident[:]
                     )
                 nc.vector.tensor_tensor(
-                    out=h_grouped[:, inner],
+                    out=h_grouped[:, b],
                     in0=turned[:].rearrange("p (t r) -> p r t", t=PACK),
                     in1=gain_col.unsqueeze(1).to_broadcast([P, P, PACK]),
                     op=ALU.mult,
                 )
-            h_codes = packed.tile([P, STEP * P], U32, align_bytes=64)
-            h_scales = packed.tile([P, STEP * P], U8, align_bytes=64)
+            h_codes = packed.tile([P, BATCH * P], U32, align_bytes=64)
+            h_scales = packed.tile([P, BATCH * P], U8, align_bytes=64)
             nc.vector.quantize_mx(
                 out=h_codes[:].bitcast(FP8X4),
                 scales=h_scales[:],
@@ -215,93 +238,96 @@ def tile_prenormtransformer_pa_t_kernel(tc, x, gains1, WQ, WK, WV, out_0, out_1,
             )
             return h_codes, h_scales
 
-        def mx_pass(out, lhs, name, cols, start, stop):
+        def mx_pass(out, lhs, b, name, cols):
             nc.tensor.matmul_mx(
                 out=out,
-                lhsT=lhs[0].bitcast(FP8X4),
-                lhsT_scale=lhs[1],
-                rhs=w_codes[name][:, cols].bitcast(FP8X4),
-                rhs_scale=w_scales[name][:, cols],
-                start=start,
-                stop=stop,
+                lhsT=lhs[0][:, b * P : (b + 1) * P].bitcast(FP8X4),
+                lhsT_scale=lhs[1][:, b * P : (b + 1) * P],
+                rhs=codes_of[name][:, cols].bitcast(FP8X4),
+                rhs_scale=scales_of[name][:, cols],
+                start=True,
+                stop=True,
             )
 
-        def project_tile(lhs, slot, i, stage_qk, stage_v):
-            everything = slice(0, FEAT)
-            odd_rows = slice(0, HALF)
-            even_rows = slice(HALF, FEAT)
-            swapped = {}
-            for name in ("q", "k"):
-                bank = psum_acc.tile([P, FEAT], F32, tag="acc", name="swapped_" + name)
-                mx_pass(bank[:], lhs, name, everything, True, True)
-                swapped[name] = bank
-            sums = psum_acc.tile([P, FEAT], F32, tag="acc")
-            for w, name in enumerate(("q", "k")):
-                mx_pass(sums[:, w * HALF : (w + 1) * HALF], lhs, name, odd_rows, True, False)
-                mx_pass(sums[:, w * HALF : (w + 1) * HALF], lhs, name, even_rows, False, True)
-            values = psum_acc.tile([P, FEAT], F32, tag="acc")
-            mx_pass(values[:], lhs, "v", everything, True, True)
-
-            mixed = rope.tile([P, 2 * HEADS, PAIRS, 2], F32)
-            for w, name in enumerate(("q", "k")):
-                nc.vector.tensor_tensor(
-                    out=mixed[:, w * HEADS : (w + 1) * HEADS],
-                    in0=swapped[name][:].rearrange("p (e h j) -> p h j e", e=2, h=HEADS),
-                    in1=mix_tab[:, slot].unsqueeze(1).to_broadcast([P, HEADS, PAIRS, 2]),
-                    op=ALU.mult,
+        def project_slot(lhs, slot, i, stage_qk, stage_v):
+            turned_by_cos = rope.tile([P, PAIRS, LANES, 2], F32)
+            rotated = rope.tile([P, PAIRS, LANES, 2], F32)
+            for c in range(QUARTERS):
+                cols = slice(c * QCOLS, (c + 1) * QCOLS)
+                straight = psum.tile([P, FEAT], F32, tag="raw")
+                crossed = psum.tile([P, FEAT], F32, tag="rot")
+                for b in range(BATCH):
+                    mx_pass(straight[:, b * QCOLS : (b + 1) * QCOLS], lhs, b, "straight", cols)
+                    mx_pass(crossed[:, b * QCOLS : (b + 1) * QCOLS], lhs, b, "crossed", cols)
+                straight_v = straight[:].rearrange("p (a m e) -> p a m e", a=LANES, e=2)
+                crossed_v = crossed[:].rearrange("p (a m e) -> p a m e", a=LANES, e=2)
+                if c in VECTOR_QUARTERS:
+                    nc.vector.tensor_tensor(
+                        out=turned_by_cos[:, c:PAIRS:QUARTERS],
+                        in0=straight_v.rearrange("p a m e -> p m a e"),
+                        in1=cos_tab[:, slot, c:PAIRS:QUARTERS].unsqueeze(2).unsqueeze(3).to_broadcast(
+                            [P, PER_QUARTER, LANES, 2]
+                        ),
+                        op=ALU.mult,
+                    )
+                else:
+                    for m in range(PER_QUARTER):
+                        j = QUARTERS * m + c
+                        nc.scalar.activation(
+                            out=turned_by_cos[:, j], in_=straight_v[:, :, m, :], func=ACT.Copy,
+                            scale=cos_tab[:, slot, j : j + 1],
+                        )
+                for m in range(PER_QUARTER):
+                    j = QUARTERS * m + c
+                    nc.vector.scalar_tensor_tensor(
+                        out=rotated[:, j], in0=crossed_v[:, :, m, :], scalar=sin_tab[:, slot, j : j + 1],
+                        in1=turned_by_cos[:, j], op0=ALU.mult, op1=ALU.add,
+                    )
+            for b in range(BATCH):
+                values = psum.tile([P, FEAT], F32, tag="val")
+                mx_pass(values[:], lhs, b, "v", slice(0, FEAT))
+                nc.scalar.copy(
+                    out=stage_v[:, b, :, i, :], in_=values[:].rearrange("p (h d) -> p h d", h=HEADS)
                 )
-            shared = rope.tile([P, 2 * HEADS, PAIRS], F32)
-            nc.vector.tensor_tensor(
-                out=shared[:],
-                in0=sums[:].rearrange("p (a j) -> p a j", j=PAIRS),
-                in1=cos_tab[:, slot].unsqueeze(1).to_broadcast([P, 2 * HEADS, PAIRS]),
-                op=ALU.mult,
-            )
-            nc.gpsimd.tensor_tensor(
-                out=stage_qk[:, :, i, :].rearrange("p a (j e) -> p a j e", e=2),
-                in0=mixed[:],
-                in1=shared[:].unsqueeze(3).to_broadcast([P, 2 * HEADS, PAIRS, 2]),
-                op=ALU.add,
-            )
-            nc.scalar.copy(
-                out=stage_v[:, :, i, :], in_=values[:].rearrange("p (h d) -> p h d", h=HEADS)
-            )
+            for b in range(BATCH):
+                for w in range(2):
+                    lanes = slice(b * QK + w * HEADS, b * QK + (w + 1) * HEADS)
+                    nc.gpsimd.tensor_scalar(
+                        out=stage_qk[:, b, w * HEADS : (w + 1) * HEADS, i, :].rearrange(
+                            "p a (j e) -> p a j e", e=2
+                        ),
+                        in0=rotated[:, :, lanes, :].rearrange("p j a e -> p a j e"),
+                        scalar1=1.0, scalar2=0.0, op0=ALU.mult, op1=ALU.add,
+                    )
 
-        def store(dst, b, first, src):
+        def store(dst, b, s, src):
+            run = RUNS[s]
             nc.sync.dma_start(
-                out=dst[b, :, first : first + GROUP, :].rearrange("h (p i) d -> p h (i d)", i=RUN),
+                out=dst[b, :, firsts[s] : firsts[s] + P * run, :].rearrange("h (p i) d -> p h (i d)", i=run),
                 in_=src.rearrange("p h i d -> p h (i d)"),
             )
 
+        slots = [(s, i) for s in range(len(RUNS)) for i in range(RUNS[s])]
         ready = {}
 
-        def prepare(step):
-            ready[step] = quantise_step(step)
-            g = step // STEPS_PER_GROUP
-            if step % STEPS_PER_GROUP == 0 and g + 1 < GROUPS:
-                group_stats(g + 1)
+        def prepare(n):
+            s, i = slots[n]
+            ready[n] = quantise_slot(s, i)
+            if i == 0 and s + 1 < len(RUNS):
+                span_stats(s + 1)
 
-        for step in range(AHEAD):
-            prepare(step)
-        stages = {}
-        for step in range(STEPS):
-            g = step // STEPS_PER_GROUP
-            if step + AHEAD < STEPS:
-                prepare(step + AHEAD)
-            if step % STEPS_PER_GROUP == 0:
-                stage_qk = stage.tile([P, 2 * HEADS, RUN, HEAD_DIM], F32)
-                stage_v = stage.tile([P, HEADS, RUN, HEAD_DIM], F32)
-                stages[g] = (stage_qk, stage_v)
-            stage_qk, stage_v = stages[g]
-            h_codes, h_scales = ready[step]
-            for inner in range(STEP):
-                i = (step % STEPS_PER_GROUP) * STEP + inner
-                cols = slice(inner * P, (inner + 1) * P)
-                slot = (g % GROUPS_PER_BATCH) * RUN + i
-                project_tile((h_codes[:, cols], h_scales[:, cols]), slot, i, stage_qk, stage_v)
-            if (step + 1) % STEPS_PER_GROUP == 0:
-                b = g // GROUPS_PER_BATCH
-                first = (g % GROUPS_PER_BATCH) * GROUP
-                store(out_2, b, first, stage_v[:])
-                store(out_0, b, first, stage_qk[:, 0:HEADS])
-                store(out_1, b, first, stage_qk[:, HEADS : 2 * HEADS])
+        for n in range(AHEAD):
+            prepare(n)
+        for n in range(SLOTS):
+            s, i = slots[n]
+            if n + AHEAD < SLOTS:
+                prepare(n + AHEAD)
+            if i == 0:
+                stage_qk = stage.tile([P, BATCH, QK, RUNS[s], HEAD_DIM], F32)
+                stage_v = stage.tile([P, BATCH, HEADS, RUNS[s], HEAD_DIM], F32)
+            project_slot(ready[n], n, i, stage_qk, stage_v)
+            if i == RUNS[s] - 1:
+                for b in range(BATCH):
+                    store(out_2, b, s, stage_v[:, b])
+                    store(out_0, b, s, stage_qk[:, b, 0:HEADS])
+                    store(out_1, b, s, stage_qk[:, b, HEADS:QK])

@@ -20,7 +20,7 @@ HALF = FEAT // 2
 EPS = 1e-5
 ROPE_THETA = 10000.0
 PACK = 4
-RUNS = (4, 4, 4, 4)
+RUNS = (2, 4, 4, 4, 2)
 SLOTS = sum(RUNS)
 QK = 2 * HEADS
 LANES = BATCH * QK
@@ -28,7 +28,7 @@ QUARTERS = 4
 PER_QUARTER = PAIRS // QUARTERS
 QCOLS = QK * PER_QUARTER * 2
 VECTOR_QUARTERS = (3,)
-AHEAD = 2
+FIRST_ROWS = 2
 ROUND_MAGIC = 1.5 * 2.0**23
 
 FLOPS = 2 * BATCH * SEQ * FEAT * 3 * FEAT
@@ -41,9 +41,9 @@ def tile_prenormtransformer_pa_t_kernel(tc, x, gains1, WQ, WK, WV, out_0, out_1,
         const = ctx.enter_context(tc.tile_pool(name="const", bufs=1))
         setup = ctx.enter_context(tc.tile_pool(name="setup", bufs=1))
         wload = ctx.enter_context(tc.tile_pool(name="wload", bufs=2))
-        small = ctx.enter_context(tc.tile_pool(name="small", bufs=3))
+        small = ctx.enter_context(tc.tile_pool(name="small", bufs=6))
         norm = ctx.enter_context(tc.tile_pool(name="norm", bufs=4))
-        packed = ctx.enter_context(tc.tile_pool(name="packed", bufs=AHEAD + 2))
+        packed = ctx.enter_context(tc.tile_pool(name="packed", bufs=3))
         rope = ctx.enter_context(tc.tile_pool(name="rope", bufs=2))
         stage = ctx.enter_context(tc.tile_pool(name="stage", bufs=2))
         psum = ctx.enter_context(tc.psum_pool(name="psum", bufs=2))
@@ -51,31 +51,41 @@ def tile_prenormtransformer_pa_t_kernel(tc, x, gains1, WQ, WK, WV, out_0, out_1,
         firsts = [P * sum(RUNS[:s]) for s in range(len(RUNS))]
         x_spans = []
 
-        def load_span(s):
-            run = RUNS[s]
-            x_span = const.tile([P, BATCH, run * FEAT], BF16, name="x_span%d" % s)
+        for s, run in enumerate(RUNS):
+            x_span = const.tile([P, BATCH, run, FEAT], BF16, name="x_span%d" % s)
+            x_spans.append(x_span)
+
+        def load_rows(s, rows):
             for b in range(BATCH):
                 nc.sync.dma_start(
-                    out=x_span[:, b, :],
-                    in_=x[b, firsts[s] : firsts[s] + P * run, :].rearrange("(p i) k -> p (i k)", i=run),
+                    out=x_spans[s][:, b, rows, :],
+                    in_=x[b, firsts[s] : firsts[s] + P * RUNS[s], :].rearrange(
+                        "(p i) k -> p i k", i=RUNS[s]
+                    )[:, rows, :],
                 )
-            x_spans.append(x_span)
 
         gain_rows = setup.tile([P, FEAT], BF16)
         nc.vector.memset(gain_rows[:], 0.0)
-        nc.scalar.dma_start(out=gain_rows[0:1, :], in_=gains1.unsqueeze(0))
-        load_span(0)
+        nc.sync.dma_start(out=gain_rows[0:1, :], in_=gains1.unsqueeze(0))
+        load_rows(0, slice(0, FIRST_ROWS))
         raw = {}
         for name, w in (("q", WQ), ("k", WK)):
             w_raw = const.tile([P, QUARTERS, FEAT], BF16, name="raw_" + name)
-            view = w.rearrange("(m c e) k -> e m c k", c=QUARTERS, e=2)
-            for e in range(2):
-                nc.sync.dma_start(out=w_raw[e:P:2], in_=view[e])
+            view = w.rearrange("(l m c e) k -> l e m c k", l=2, c=QUARTERS, e=2)
+            for l in range(2):
+                for e in range(2):
+                    nc.sync.dma_start(out=w_raw[2 * l + e : P : 4], in_=view[l, e])
             raw[name] = w_raw
         v_raw = const.tile([P, PACK, FEAT], BF16)
         nc.sync.dma_start(out=v_raw[:], in_=WV.rearrange("(c p) k -> p c k", p=P))
         for s in range(1, len(RUNS)):
-            load_span(s)
+            load_rows(s, slice(0, RUNS[s]))
+
+        warm = setup.tile([P, 1], F32)
+        nc.vector.memset(warm[:], 0.0)
+        nc.scalar.activation(out=warm[:], in_=warm[:], func=ACT.Sin)
+        minus_half = const.tile([P, 2 * BATCH], F32)
+        nc.gpsimd.memset(minus_half[:], -0.5)
 
         ident = const.tile([P, P], F32)
         make_identity(nc, ident[:])
@@ -91,16 +101,18 @@ def tile_prenormtransformer_pa_t_kernel(tc, x, gains1, WQ, WK, WV, out_0, out_1,
             out=sign[:], in0=odd_int[:], scalar1=-2.0, scalar2=1.0, op0=ALU.mult, op1=ALU.add
         )
 
-        pos_int = setup.tile([P, SLOTS], I32)
+        pos = setup.tile([P, SLOTS], F32)
         slot0 = 0
         for s, run in enumerate(RUNS):
             nc.gpsimd.iota(
-                pos_int[:, slot0 : slot0 + run], pattern=[[1, run]], base=firsts[s], channel_multiplier=run
+                pos[:, slot0 : slot0 + run], pattern=[[1, run]], base=firsts[s], channel_multiplier=run,
+                allow_small_or_imprecise_dtypes=True,
             )
             slot0 += run
-        pos = setup.tile([P, SLOTS], F32)
-        nc.vector.tensor_copy(out=pos[:], in_=pos_int[:])
         turns = setup.tile([P, 2, SLOTS, PAIRS], F32)
+        sin_cos = const.tile([P, 2, SLOTS, PAIRS], F32)
+        sin_tab = sin_cos[:, 0]
+        cos_tab = sin_cos[:, 1]
         for j in range(PAIRS):
             nc.vector.tensor_scalar(
                 out=turns[:, 0, :, j],
@@ -109,20 +121,21 @@ def tile_prenormtransformer_pa_t_kernel(tc, x, gains1, WQ, WK, WV, out_0, out_1,
                 scalar2=None,
                 op0=ALU.mult,
             )
-        nc.vector.tensor_scalar(
-            out=turns[:, 1], in0=turns[:, 0], scalar1=0.25, scalar2=None, op0=ALU.add
-        )
-        whole = setup.tile([P, 2, SLOTS, PAIRS], F32)
-        nc.vector.tensor_scalar(
-            out=whole[:], in0=turns[:], scalar1=ROUND_MAGIC, scalar2=ROUND_MAGIC,
-            op0=ALU.add, op1=ALU.subtract,
-        )
-        part = setup.tile([P, 2, SLOTS, PAIRS], F32)
-        nc.vector.tensor_tensor(out=part[:], in0=turns[:], in1=whole[:], op=ALU.subtract)
-        sin_cos = const.tile([P, 2, SLOTS, PAIRS], F32)
-        nc.scalar.activation(out=sin_cos[:], in_=part[:], func=ACT.Sin, scale=2.0 * math.pi)
-        sin_tab = sin_cos[:, 0]
-        cos_tab = sin_cos[:, 1]
+
+        def make_tables(rows):
+            nc.vector.tensor_scalar(
+                out=turns[:, 1, rows], in0=turns[:, 0, rows], scalar1=0.25, scalar2=None, op0=ALU.add
+            )
+            whole = setup.tile([P, 2, rows.stop - rows.start, PAIRS], F32)
+            nc.vector.tensor_scalar(
+                out=whole[:], in0=turns[:, :, rows], scalar1=ROUND_MAGIC, scalar2=ROUND_MAGIC,
+                op0=ALU.add, op1=ALU.subtract,
+            )
+            part = setup.tile([P, 2, rows.stop - rows.start, PAIRS], F32)
+            nc.vector.tensor_tensor(out=part[:], in0=turns[:, :, rows], in1=whole[:], op=ALU.subtract)
+            nc.scalar.activation(out=sin_cos[:, :, rows], in_=part[:], func=ACT.Sin, scale=2.0 * math.pi)
+
+        make_tables(slice(0, RUNS[0]))
 
         gain_bank = psum.tile([P, FEAT], F32, tag="val")
         for u in range(2):
@@ -133,34 +146,95 @@ def tile_prenormtransformer_pa_t_kernel(tc, x, gains1, WQ, WK, WV, out_0, out_1,
         nc.vector.tensor_copy(out=gain_words[:], in_=gain_bank[:, 0 : 2 * P : P])
         gain_col = gain_words[:].bitcast(BF16)
 
+        slots = [(s, i) for s in range(len(RUNS)) for i in range(RUNS[s])]
+        sums_of = {}
         rstd_of = {}
 
-        def span_stats(s):
-            n = BATCH * RUNS[s]
-            squares = norm.tile([P, FEAT], BF16, tag="squares", bufs=2)
-            sumsq = small.tile([P, n], F32)
+        def square_slot(n):
+            if n % 2 == 0:
+                sums_of[n // 2] = small.tile([P, 2, BATCH], F32, name="sumsq")
+            s, i = slots[n]
             for b in range(BATCH):
-                for i in range(RUNS[s]):
-                    nc.scalar.activation(
-                        out=squares[:], in_=x_spans[s][:, b, i * FEAT : (i + 1) * FEAT], func=ACT.Square,
-                        accum_out=sumsq[:, b * RUNS[s] + i : b * RUNS[s] + i + 1],
-                    )
-            meansq = small.tile([P, n], F32)
-            nc.vector.tensor_scalar(
-                out=meansq[:], in0=sumsq[:], scalar1=1.0 / FEAT, scalar2=EPS, op0=ALU.mult, op1=ALU.add
+                squares = norm.tile([P, FEAT], BF16, tag="squares", bufs=2)
+                nc.scalar.activation(
+                    out=squares[:], in_=x_spans[s][:, b, i, :], func=ACT.Square,
+                    accum_out=sums_of[n // 2][:, n % 2, b : b + 1],
+                )
+
+        def finish_slots(n, count):
+            sums = sums_of[n // 2][:, n % 2 : n % 2 + count].rearrange("p k b -> p (k b)")
+            meansq = small.tile([P, count * BATCH], F32)
+            nc.gpsimd.tensor_scalar(
+                out=meansq[:], in0=sums, scalar1=1.0 / FEAT, scalar2=EPS, op0=ALU.mult, op1=ALU.add
             )
-            rms = small.tile([P, n], F32)
-            nc.scalar.activation(out=rms[:], in_=meansq[:], func=ACT.Sqrt)
-            rstd = small.tile([P, n], F32)
-            nc.vector.reciprocal(out=rstd[:], in_=rms[:])
-            rstd_of[s] = rstd
+            rstd = small.tile([P, count * BATCH], F32)
+            nc.gpsimd.tensor_tensor(
+                out=rstd[:], in0=meansq[:], in1=minus_half[:, 0 : count * BATCH], op=ALU.pow
+            )
+            for k in range(count):
+                rstd_of[n + k] = rstd[:, k * BATCH : (k + 1) * BATCH]
 
-        span_stats(0)
+        scaled_of = {}
+        grouped_of = {}
+        turned_of = {}
+        packed_of = {}
 
+        def norm_slot(n):
+            s, i = slots[n]
+            scaled_of[n] = []
+            for b in range(BATCH):
+                scaled = norm.tile([P, FEAT], F32, bufs=6)
+                sorted_out = scaled[:].rearrange("p (t q) -> p t q", t=PACK)
+                sorted_in = x_spans[s][:, b, i, :].rearrange("p (q t) -> p t q", t=PACK)
+                if b == 1:
+                    nc.scalar.activation(
+                        out=sorted_out, in_=sorted_in, func=ACT.Copy, scale=rstd_of[n][:, b : b + 1]
+                    )
+                else:
+                    nc.gpsimd.tensor_scalar(
+                        out=sorted_out, in0=sorted_in, scalar1=rstd_of[n][:, b : b + 1], scalar2=0.0,
+                        op0=ALU.mult, op1=ALU.add,
+                    )
+                scaled_of[n].append(scaled)
+
+        def turn_slot(n):
+            turned_of[n] = []
+            for b in range(BATCH):
+                turned = psum.tile([P, FEAT], F32, tag="turn")
+                for t in range(PACK):
+                    cols = slice(t * P, (t + 1) * P)
+                    nc.tensor.transpose(turned[:, cols], scaled_of[n][b][:, cols], ident[:])
+                turned_of[n].append(turned)
+            grouped_of[n] = norm.tile([P, BATCH, P, PACK], BF16, align_bytes=64, bufs=3, name="h_grouped")
+
+        def gain_slot(n, b):
+            nc.vector.tensor_tensor(
+                out=grouped_of[n][:, b],
+                in0=turned_of[n][b][:].rearrange("p (t r) -> p r t", t=PACK),
+                in1=gain_col.unsqueeze(1).to_broadcast([P, P, PACK]),
+                op=ALU.mult,
+            )
+
+        def quantise_slot(n):
+            h_codes = packed.tile([P, BATCH * P], U32, align_bytes=64)
+            h_scales = packed.tile([P, BATCH * P], U8, align_bytes=64)
+            nc.vector.quantize_mx(
+                out=h_codes[:].bitcast(FP8X4),
+                scales=h_scales[:],
+                in_=grouped_of[n][:].rearrange("p a r t -> p (a r t)"),
+            )
+            packed_of[n] = (h_codes, h_scales)
+
+        square_slot(0)
+        finish_slots(0, 1)
+        norm_slot(0)
+        square_slot(1)
+        finish_slots(1, 1)
+        norm_slot(1)
         turns_of_copies = [0]
 
         def copy_out(out, in_):
-            if turns_of_copies[0] % 2 == 0:
+            if turns_of_copies[0] > 4 and turns_of_copies[0] % 2 == 1:
                 nc.vector.tensor_copy(out=out, in_=in_)
             else:
                 nc.scalar.copy(out=out, in_=in_)
@@ -184,59 +258,31 @@ def tile_prenormtransformer_pa_t_kernel(tc, x, gains1, WQ, WK, WV, out_0, out_1,
         for name, width in (("straight", QUARTERS * QCOLS), ("crossed", QUARTERS * QCOLS), ("v", FEAT)):
             codes_of[name] = const.tile([P, width], U32, name="codes_" + name, align_bytes=64)
             scales_of[name] = const.tile([P, width], U8, name="scales_" + name, align_bytes=64)
-        signed = {}
-        for name in ("q", "k"):
-            w_signed = const.tile([P, QUARTERS, FEAT], BF16, name="signed_" + name)
-            nc.vector.tensor_scalar(
-                out=w_signed[:], in0=raw[name][:], scalar1=sign[:], scalar2=None, op0=ALU.mult
-            )
-            signed[name] = w_signed
-        for c in range(QUARTERS):
-            cols = slice(c * QCOLS, (c + 1) * QCOLS)
-            for name, source, matrix, tag in (
-                ("straight", raw, ident, "raw"), ("crossed", signed, swap, "rot")
+        def prepare_quarter(c):
+            straight = [raw[name][:, c, :].bitcast(F32) for name in ("q", "k")]
+            crossed = []
+            for name in ("q", "k"):
+                w_signed = wload.tile([P, FEAT], BF16, bufs=4, name="w_signed")
+                nc.vector.tensor_scalar(
+                    out=w_signed[:], in0=raw[name][:, c, :], scalar1=sign[:], scalar2=None, op0=ALU.mult
+                )
+                crossed.append(w_signed[:].bitcast(F32))
+            for name, chunks, matrix, tag in (
+                ("straight", straight, ident, "raw"), ("crossed", crossed, swap, "rot")
             ):
                 w_grouped = wload.tile([P, QCOLS * PACK], BF16, align_bytes=64)
                 prepare_columns(
-                    codes_of[name], scales_of[name], cols, w_grouped,
-                    [source[w][:, c, :].bitcast(F32) for w in ("q", "k")], matrix, tag,
+                    codes_of[name], scales_of[name], slice(c * QCOLS, (c + 1) * QCOLS), w_grouped,
+                    chunks, matrix, tag,
                 )
-        for c in range(2):
-            w_grouped = wload.tile([P, QCOLS * PACK], BF16, align_bytes=64)
-            prepare_columns(
-                codes_of["v"], scales_of["v"], slice(c * QCOLS, (c + 1) * QCOLS), w_grouped,
-                [v_raw[:, 2 * c + n, :].bitcast(F32) for n in range(2)], ident, "val",
-            )
 
-        def quantise_slot(s, i):
-            h_grouped = norm.tile([P, BATCH, P, PACK], BF16, align_bytes=64)
-            for b in range(BATCH):
-                scaled = norm.tile([P, FEAT], F32)
-                col = b * RUNS[s] + i
-                nc.gpsimd.tensor_scalar(
-                    out=scaled[:].rearrange("p (t q) -> p t q", t=PACK),
-                    in0=x_spans[s][:, b, i * FEAT : (i + 1) * FEAT].rearrange("p (q t) -> p t q", t=PACK),
-                    scalar1=rstd_of[s][:, col : col + 1], scalar2=0.0, op0=ALU.mult, op1=ALU.add,
+        def prepare_values():
+            for c in range(2):
+                w_grouped = wload.tile([P, QCOLS * PACK], BF16, align_bytes=64)
+                prepare_columns(
+                    codes_of["v"], scales_of["v"], slice(c * QCOLS, (c + 1) * QCOLS), w_grouped,
+                    [v_raw[:, 2 * c + n, :].bitcast(F32) for n in range(2)], ident, "val",
                 )
-                turned = psum.tile([P, FEAT], F32, tag="turn")
-                for t in range(PACK):
-                    nc.tensor.transpose(
-                        turned[:, t * P : (t + 1) * P], scaled[:, t * P : (t + 1) * P], ident[:]
-                    )
-                nc.vector.tensor_tensor(
-                    out=h_grouped[:, b],
-                    in0=turned[:].rearrange("p (t r) -> p r t", t=PACK),
-                    in1=gain_col.unsqueeze(1).to_broadcast([P, P, PACK]),
-                    op=ALU.mult,
-                )
-            h_codes = packed.tile([P, BATCH * P], U32, align_bytes=64)
-            h_scales = packed.tile([P, BATCH * P], U8, align_bytes=64)
-            nc.vector.quantize_mx(
-                out=h_codes[:].bitcast(FP8X4),
-                scales=h_scales[:],
-                in_=h_grouped[:].rearrange("p a r t -> p (a r t)"),
-            )
-            return h_codes, h_scales
 
         def mx_pass(out, lhs, b, name, cols):
             nc.tensor.matmul_mx(
@@ -249,56 +295,71 @@ def tile_prenormtransformer_pa_t_kernel(tc, x, gains1, WQ, WK, WV, out_0, out_1,
                 stop=True,
             )
 
-        def project_slot(lhs, slot, i, stage_qk, stage_v):
-            turned_by_cos = rope.tile([P, PAIRS, LANES, 2], F32)
-            rotated = rope.tile([P, PAIRS, LANES, 2], F32)
-            for c in range(QUARTERS):
-                cols = slice(c * QCOLS, (c + 1) * QCOLS)
-                straight = psum.tile([P, FEAT], F32, tag="raw")
-                crossed = psum.tile([P, FEAT], F32, tag="rot")
-                for b in range(BATCH):
-                    mx_pass(straight[:, b * QCOLS : (b + 1) * QCOLS], lhs, b, "straight", cols)
-                    mx_pass(crossed[:, b * QCOLS : (b + 1) * QCOLS], lhs, b, "crossed", cols)
-                straight_v = straight[:].rearrange("p (a m e) -> p a m e", a=LANES, e=2)
-                crossed_v = crossed[:].rearrange("p (a m e) -> p a m e", a=LANES, e=2)
-                if c in VECTOR_QUARTERS:
-                    nc.vector.tensor_tensor(
-                        out=turned_by_cos[:, c:PAIRS:QUARTERS],
-                        in0=straight_v.rearrange("p a m e -> p m a e"),
-                        in1=cos_tab[:, slot, c:PAIRS:QUARTERS].unsqueeze(2).unsqueeze(3).to_broadcast(
-                            [P, PER_QUARTER, LANES, 2]
-                        ),
-                        op=ALU.mult,
-                    )
-                else:
-                    for m in range(PER_QUARTER):
-                        j = QUARTERS * m + c
-                        nc.scalar.activation(
-                            out=turned_by_cos[:, j], in_=straight_v[:, :, m, :], func=ACT.Copy,
-                            scale=cos_tab[:, slot, j : j + 1],
-                        )
+        banks = {}
+        cos_part = {}
+        rotated_of = {}
+
+        def project_quarter(n, c):
+            cols = slice(c * QCOLS, (c + 1) * QCOLS)
+            straight = psum.tile([P, FEAT], F32, tag="raw")
+            crossed = psum.tile([P, FEAT], F32, tag="rot")
+            for b in range(BATCH):
+                mx_pass(straight[:, b * QCOLS : (b + 1) * QCOLS], packed_of[n], b, "straight", cols)
+                mx_pass(crossed[:, b * QCOLS : (b + 1) * QCOLS], packed_of[n], b, "crossed", cols)
+            banks[c] = [bank[:].rearrange("p (g m f) -> p g m f", m=PER_QUARTER, f=4) for bank in (straight, crossed)]
+
+        def cosine_quarter(n, c):
+            if c == 0:
+                cos_part[n] = rope.tile([P, LANES // 2, PAIRS, 4], F32, name="turned_by_cos")
+                rotated_of[n] = rope.tile([P, LANES // 2, PAIRS, 4], F32, name="rotated")
+            straight = banks[c][0]
+            if c in VECTOR_QUARTERS:
+                nc.vector.tensor_tensor(
+                    out=cos_part[n][:, :, c:PAIRS:QUARTERS, :],
+                    in0=straight,
+                    in1=cos_tab[:, n, c:PAIRS:QUARTERS].unsqueeze(1).unsqueeze(3).to_broadcast(
+                        [P, LANES // 2, PER_QUARTER, 4]
+                    ),
+                    op=ALU.mult,
+                )
+            else:
                 for m in range(PER_QUARTER):
                     j = QUARTERS * m + c
-                    nc.vector.scalar_tensor_tensor(
-                        out=rotated[:, j], in0=crossed_v[:, :, m, :], scalar=sin_tab[:, slot, j : j + 1],
-                        in1=turned_by_cos[:, j], op0=ALU.mult, op1=ALU.add,
+                    nc.scalar.activation(
+                        out=cos_part[n][:, :, j, :], in_=straight[:, :, m, :], func=ACT.Copy,
+                        scale=cos_tab[:, n, j : j + 1],
                     )
+
+        def sine_quarter(n, c):
+            for m in range(PER_QUARTER):
+                j = QUARTERS * m + c
+                nc.vector.scalar_tensor_tensor(
+                    out=rotated_of[n][:, :, j, :], in0=banks[c][1][:, :, m, :],
+                    scalar=sin_tab[:, n, j : j + 1], in1=cos_part[n][:, :, j, :],
+                    op0=ALU.mult, op1=ALU.add,
+                )
+
+        def project_values(n):
+            banks["v"] = []
             for b in range(BATCH):
                 values = psum.tile([P, FEAT], F32, tag="val")
-                mx_pass(values[:], lhs, b, "v", slice(0, FEAT))
-                nc.scalar.copy(
-                    out=stage_v[:, b, :, i, :], in_=values[:].rearrange("p (h d) -> p h d", h=HEADS)
+                mx_pass(values[:], packed_of[n], b, "v", slice(0, FEAT))
+                banks["v"].append(values)
+
+        def copy_values(i, b, stage_v):
+            nc.scalar.copy(
+                out=stage_v[:, b, :, i, :], in_=banks["v"][b][:].rearrange("p (h d) -> p h d", h=HEADS)
+            )
+
+        def sort_slot(n, i, stage_qk):
+            for l in range(2):
+                nc.gpsimd.tensor_scalar(
+                    out=stage_qk[:, :, :, i, :].rearrange(
+                        "p b (w l h) (j e) -> p (b w) l h j e", w=2, l=2, e=2
+                    )[:, :, l],
+                    in0=rotated_of[n][:].rearrange("p (a h) j (l e) -> p a h j l e", h=4, l=2)[:, :, :, :, l, :],
+                    scalar1=1.0, scalar2=0.0, op0=ALU.mult, op1=ALU.add,
                 )
-            for b in range(BATCH):
-                for w in range(2):
-                    lanes = slice(b * QK + w * HEADS, b * QK + (w + 1) * HEADS)
-                    nc.gpsimd.tensor_scalar(
-                        out=stage_qk[:, b, w * HEADS : (w + 1) * HEADS, i, :].rearrange(
-                            "p a (j e) -> p a j e", e=2
-                        ),
-                        in0=rotated[:, :, lanes, :].rearrange("p j a e -> p a j e"),
-                        scalar1=1.0, scalar2=0.0, op0=ALU.mult, op1=ALU.add,
-                    )
 
         def store(dst, b, s, src):
             run = RUNS[s]
@@ -307,25 +368,49 @@ def tile_prenormtransformer_pa_t_kernel(tc, x, gains1, WQ, WK, WV, out_0, out_1,
                 in_=src.rearrange("p h i d -> p h (i d)"),
             )
 
-        slots = [(s, i) for s in range(len(RUNS)) for i in range(RUNS[s])]
-        ready = {}
-
-        def prepare(n):
-            s, i = slots[n]
-            ready[n] = quantise_slot(s, i)
-            if i == 0 and s + 1 < len(RUNS):
-                span_stats(s + 1)
-
-        for n in range(AHEAD):
-            prepare(n)
+        prepare_quarter(0)
+        turn_slot(0)
+        for b in range(BATCH):
+            gain_slot(0, b)
+        quantise_slot(0)
         for n in range(SLOTS):
             s, i = slots[n]
-            if n + AHEAD < SLOTS:
-                prepare(n + AHEAD)
+            more = n + 1 < SLOTS
             if i == 0:
                 stage_qk = stage.tile([P, BATCH, QK, RUNS[s], HEAD_DIM], F32)
                 stage_v = stage.tile([P, BATCH, HEADS, RUNS[s], HEAD_DIM], F32)
-            project_slot(ready[n], n, i, stage_qk, stage_v)
+            for c in range(QUARTERS):
+                if n == 0 and c > 0:
+                    prepare_quarter(c)
+                if n == 0 and c == 2:
+                    make_tables(slice(RUNS[0], SLOTS))
+                if c == 3:
+                    if n == 0:
+                        prepare_values()
+                    project_values(n)
+                project_quarter(n, c)
+                if c == 1 and more:
+                    turn_slot(n + 1)
+                cosine_quarter(n, c)
+                sine_quarter(n, c)
+                if c == 1 and more:
+                    gain_slot(n + 1, 0)
+                if c == 2 and more:
+                    gain_slot(n + 1, 1)
+                    quantise_slot(n + 1)
+            for b in range(BATCH):
+                copy_values(i, b, stage_v)
+            if n == 0:
+                square_slot(2)
+                square_slot(3)
+                finish_slots(2, 2)
+            if n + 4 < SLOTS:
+                square_slot(n + 4)
+                if n % 2 == 1:
+                    finish_slots(n + 3, 2)
+            sort_slot(n, i, stage_qk)
+            if n + 2 < SLOTS:
+                norm_slot(n + 2)
             if i == RUNS[s] - 1:
                 for b in range(BATCH):
                     store(out_2, b, s, stage_v[:, b])

import math
from contextlib import ExitStack

import concourse.mybir as mybir
from concourse.masks import make_identity

F32 = mybir.dt.float32
BF16 = mybir.dt.bfloat16
I32 = mybir.dt.int32
U32 = mybir.dt.uint32
U8 = mybir.dt.uint8
FP8X4 = mybir.dt.float8_e4m3fn_x4
ALU = mybir.AluOpType
ACT = mybir.ActivationFunctionType

P = 128
BATCH, SEQ, FEAT, HEADS, HEAD_DIM = 2, 2048, 512, 8, 64
PAIRS = HEAD_DIM // 2
HALF = FEAT // 2
EPS = 1e-5
ROPE_THETA = 10000.0
PACK = 4
RUNS = (2, 4, 4, 4, 2)
SLOTS = sum(RUNS)
QK = 2 * HEADS
LANES = BATCH * QK
QUARTERS = 4
PER_QUARTER = PAIRS // QUARTERS
QCOLS = QK * PER_QUARTER * 2
VECTOR_QUARTERS = (3,)
FIRST_ROWS = 2
ROUND_MAGIC = 1.5 * 2.0**23

FLOPS = 2 * BATCH * SEQ * FEAT * 3 * FEAT


def tile_prenormtransformer_pa_t_kernel(tc, x, gains1, WQ, WK, WV, out_0, out_1, out_2):
    nc = tc.nc

    with ExitStack() as ctx:
        const = ctx.enter_context(tc.tile_pool(name="const", bufs=1))
        setup = ctx.enter_context(tc.tile_pool(name="setup", bufs=1))
        wload = ctx.enter_context(tc.tile_pool(name="wload", bufs=2))
        small = ctx.enter_context(tc.tile_pool(name="small", bufs=6))
        norm = ctx.enter_context(tc.tile_pool(name="norm", bufs=4))
        packed = ctx.enter_context(tc.tile_pool(name="packed", bufs=3))
        rope = ctx.enter_context(tc.tile_pool(name="rope", bufs=2))
        stage = ctx.enter_context(tc.tile_pool(name="stage", bufs=2))
        psum = ctx.enter_context(tc.psum_pool(name="psum", bufs=2))

        firsts = [P * sum(RUNS[:s]) for s in range(len(RUNS))]
        x_spans = []

        for s, run in enumerate(RUNS):
            x_span = const.tile([P, BATCH, run, FEAT], BF16, name="x_span%d" % s)
            x_spans.append(x_span)

        def load_rows(s, rows):
            for b in range(BATCH):
                nc.sync.dma_start(
                    out=x_spans[s][:, b, rows, :],
                    in_=x[b, firsts[s] : firsts[s] + P * RUNS[s], :].rearrange(
                        "(p i) k -> p i k", i=RUNS[s]
                    )[:, rows, :],
                )

        gain_rows = setup.tile([P, FEAT], BF16)
        nc.vector.memset(gain_rows[:], 0.0)
        nc.sync.dma_start(out=gain_rows[0:1, :], in_=gains1.unsqueeze(0))
        load_rows(0, slice(0, FIRST_ROWS))
        raw = {}
        for name, w in (("q", WQ), ("k", WK)):
            w_raw = const.tile([P, QUARTERS, FEAT], BF16, name="raw_" + name)
            view = w.rearrange("(l m c e) k -> l e m c k", l=2, c=QUARTERS, e=2)
            for l in range(2):
                for e in range(2):
                    nc.sync.dma_start(out=w_raw[2 * l + e : P : 4], in_=view[l, e])
            raw[name] = w_raw
        v_raw = const.tile([P, PACK, FEAT], BF16)
        nc.sync.dma_start(out=v_raw[:], in_=WV.rearrange("(c p) k -> p c k", p=P))
        for s in range(1, len(RUNS)):
            load_rows(s, slice(0, RUNS[s]))

        warm = setup.tile([P, 1], F32)
        nc.vector.memset(warm[:], 0.0)
        nc.scalar.activation(out=warm[:], in_=warm[:], func=ACT.Sin)
        minus_half = const.tile([P, 2 * BATCH], F32)
        nc.gpsimd.memset(minus_half[:], -0.5)

        ident = const.tile([P, P], F32)
        make_identity(nc, ident[:])
        swap = const.tile([P, P], F32)
        nc.vector.tensor_copy(out=swap[:, 0:P:2], in_=ident[:, 1:P:2])
        nc.vector.tensor_copy(out=swap[:, 1:P:2], in_=ident[:, 0:P:2])
        part_int = setup.tile([P, 1], I32)
        nc.gpsimd.iota(part_int[:], pattern=[[0, 1]], base=0, channel_multiplier=1)
        odd_int = setup.tile([P, 1], I32)
        nc.vector.tensor_scalar(out=odd_int[:], in0=part_int[:], scalar1=1, scalar2=None, op0=ALU.bitwise_and)
        sign = setup.tile([P, 1], F32)
        nc.vector.tensor_scalar(
            out=sign[:], in0=odd_int[:], scalar1=-2.0, scalar2=1.0, op0=ALU.mult, op1=ALU.add
        )

        pos = setup.tile([P, SLOTS], F32)
        slot0 = 0
        for s, run in enumerate(RUNS):
            nc.gpsimd.iota(
                pos[:, slot0 : slot0 + run], pattern=[[1, run]], base=firsts[s], channel_multiplier=run,
                allow_small_or_imprecise_dtypes=True,
            )
            slot0 += run
        turns = setup.tile([P, 2, SLOTS, PAIRS], F32)
        sin_cos = const.tile([P, 2, SLOTS, PAIRS], F32)
        sin_tab = sin_cos[:, 0]
        cos_tab = sin_cos[:, 1]
        for j in range(PAIRS):
            nc.vector.tensor_scalar(
                out=turns[:, 0, :, j],
                in0=pos[:],
                scalar1=ROPE_THETA ** (-2.0 * j / HEAD_DIM) / (2.0 * math.pi),
                scalar2=None,
                op0=ALU.mult,
            )

        def make_tables(rows):
            nc.vector.tensor_scalar(
                out=turns[:, 1, rows], in0=turns[:, 0, rows], scalar1=0.25, scalar2=None, op0=ALU.add
            )
            whole = setup.tile([P, 2, rows.stop - rows.start, PAIRS], F32)
            nc.vector.tensor_scalar(
                out=whole[:], in0=turns[:, :, rows], scalar1=ROUND_MAGIC, scalar2=ROUND_MAGIC,
                op0=ALU.add, op1=ALU.subtract,
            )
            part = setup.tile([P, 2, rows.stop - rows.start, PAIRS], F32)
            nc.vector.tensor_tensor(out=part[:], in0=turns[:, :, rows], in1=whole[:], op=ALU.subtract)
            nc.scalar.activation(out=sin_cos[:, :, rows], in_=part[:], func=ACT.Sin, scale=2.0 * math.pi)

        make_tables(slice(0, RUNS[0]))

        gain_bank = psum.tile([P, FEAT], F32, tag="val")
        for u in range(2):
            nc.tensor.transpose(
                gain_bank[:, u * P : (u + 1) * P], gain_rows[:].bitcast(F32)[:, u:HALF:2], ident[:]
            )
        gain_words = const.tile([P, 2], F32)
        nc.vector.tensor_copy(out=gain_words[:], in_=gain_bank[:, 0 : 2 * P : P])
        gain_col = gain_words[:].bitcast(BF16)

        slots = [(s, i) for s in range(len(RUNS)) for i in range(RUNS[s])]
        sums_of = {}
        rstd_of = {}

        def square_slot(n):
            if n % 2 == 0:
                sums_of[n // 2] = small.tile([P, 2, BATCH], F32, name="sumsq")
            s, i = slots[n]
            for b in range(BATCH):
                squares = norm.tile([P, FEAT], BF16, tag="squares", bufs=2)
                nc.scalar.activation(
                    out=squares[:], in_=x_spans[s][:, b, i, :], func=ACT.Square,
                    accum_out=sums_of[n // 2][:, n % 2, b : b + 1],
                )

        def finish_slots(n, count):
            sums = sums_of[n // 2][:, n % 2 : n % 2 + count].rearrange("p k b -> p (k b)")
            meansq = small.tile([P, count * BATCH], F32)
            nc.gpsimd.tensor_scalar(
                out=meansq[:], in0=sums, scalar1=1.0 / FEAT, scalar2=EPS, op0=ALU.mult, op1=ALU.add
            )
            rstd = small.tile([P, count * BATCH], F32)
            nc.gpsimd.tensor_tensor(
                out=rstd[:], in0=meansq[:], in1=minus_half[:, 0 : count * BATCH], op=ALU.pow
            )
            for k in range(count):
                rstd_of[n + k] = rstd[:, k * BATCH : (k + 1) * BATCH]

        scaled_of = {}
        grouped_of = {}
        turned_of = {}
        packed_of = {}

        def norm_slot(n):
            s, i = slots[n]
            scaled_of[n] = []
            for b in range(BATCH):
                scaled = norm.tile([P, FEAT], F32, bufs=6)
                sorted_out = scaled[:].rearrange("p (t q) -> p t q", t=PACK)
                sorted_in = x_spans[s][:, b, i, :].rearrange("p (q t) -> p t q", t=PACK)
                if b == 1:
                    nc.scalar.activation(
                        out=sorted_out, in_=sorted_in, func=ACT.Copy, scale=rstd_of[n][:, b : b + 1]
                    )
                else:
                    nc.gpsimd.tensor_scalar(
                        out=sorted_out, in0=sorted_in, scalar1=rstd_of[n][:, b : b + 1], scalar2=0.0,
                        op0=ALU.mult, op1=ALU.add,
                    )
                scaled_of[n].append(scaled)

        def turn_slot(n):
            turned_of[n] = []
            for b in range(BATCH):
                turned = psum.tile([P, FEAT], F32, tag="turn")
                for t in range(PACK):
                    cols = slice(t * P, (t + 1) * P)
                    nc.tensor.transpose(turned[:, cols], scaled_of[n][b][:, cols], ident[:])
                turned_of[n].append(turned)
            grouped_of[n] = norm.tile([P, BATCH, P, PACK], BF16, align_bytes=64, bufs=3, name="h_grouped")

        def gain_slot(n, b):
            nc.vector.tensor_tensor(
                out=grouped_of[n][:, b],
                in0=turned_of[n][b][:].rearrange("p (t r) -> p r t", t=PACK),
                in1=gain_col.unsqueeze(1).to_broadcast([P, P, PACK]),
                op=ALU.mult,
            )

        def quantise_slot(n):
            h_codes = packed.tile([P, BATCH * P], U32, align_bytes=64)
            h_scales = packed.tile([P, BATCH * P], U8, align_bytes=64)
            nc.vector.quantize_mx(
                out=h_codes[:].bitcast(FP8X4),
                scales=h_scales[:],
                in_=grouped_of[n][:].rearrange("p a r t -> p (a r t)"),
            )
            packed_of[n] = (h_codes, h_scales)

        square_slot(0)
        finish_slots(0, 1)
        norm_slot(0)
        square_slot(1)
        finish_slots(1, 1)
        norm_slot(1)
        turns_of_copies = [0]

        def copy_out(out, in_):
            if turns_of_copies[0] > 4 and turns_of_copies[0] % 2 == 1:
                nc.vector.tensor_copy(out=out, in_=in_)
            else:
                nc.scalar.copy(out=out, in_=in_)
            turns_of_copies[0] += 1

        def prepare_columns(codes, scales, cols, w_grouped, chunks, matrix, tag):
            bank = psum.tile([P, FEAT], F32, tag=tag, name="w_bank")
            for n, chunk in enumerate(chunks):
                for u in range(2):
                    nc.tensor.transpose(
                        bank[:, (2 * n + u) * P : (2 * n + u + 1) * P], chunk[:, u:HALF:2], matrix[:]
                    )
            copy_out(
                w_grouped[:].bitcast(F32).rearrange("p (b r u) -> p b r u", b=2, u=2),
                bank[:].rearrange("p (b u r) -> p b r u", b=2, u=2),
            )
            nc.vector.quantize_mx(out=codes[:, cols].bitcast(FP8X4), scales=scales[:, cols], in_=w_grouped[:])

        codes_of = {}
        scales_of = {}
        for name, width in (("straight", QUARTERS * QCOLS), ("crossed", QUARTERS * QCOLS), ("v", FEAT)):
            codes_of[name] = const.tile([P, width], U32, name="codes_" + name, align_bytes=64)
            scales_of[name] = const.tile([P, width], U8, name="scales_" + name, align_bytes=64)
        def prepare_quarter(c):
            straight = [raw[name][:, c, :].bitcast(F32) for name in ("q", "k")]
            crossed = []
            for name in ("q", "k"):
                w_signed = wload.tile([P, FEAT], BF16, bufs=4, name="w_signed")
                nc.vector.tensor_scalar(
                    out=w_signed[:], in0=raw[name][:, c, :], scalar1=sign[:], scalar2=None, op0=ALU.mult
                )
                crossed.append(w_signed[:].bitcast(F32))
            for name, chunks, matrix, tag in (
                ("straight", straight, ident, "raw"), ("crossed", crossed, swap, "rot")
            ):
                w_grouped = wload.tile([P, QCOLS * PACK], BF16, align_bytes=64)
                prepare_columns(
                    codes_of[name], scales_of[name], slice(c * QCOLS, (c + 1) * QCOLS), w_grouped,
                    chunks, matrix, tag,
                )

        def prepare_values():
            for c in range(2):
                w_grouped = wload.tile([P, QCOLS * PACK], BF16, align_bytes=64)
                prepare_columns(
                    codes_of["v"], scales_of["v"], slice(c * QCOLS, (c + 1) * QCOLS), w_grouped,
                    [v_raw[:, 2 * c + n, :].bitcast(F32) for n in range(2)], ident, "val",
                )

        def mx_pass(out, lhs, b, name, cols):
            nc.tensor.matmul_mx(
                out=out,
                lhsT=lhs[0][:, b * P : (b + 1) * P].bitcast(FP8X4),
                lhsT_scale=lhs[1][:, b * P : (b + 1) * P],
                rhs=codes_of[name][:, cols].bitcast(FP8X4),
                rhs_scale=scales_of[name][:, cols],
                start=True,
                stop=True,
            )

        banks = {}
        cos_part = {}
        rotated_of = {}

        def project_quarter(n, c):
            cols = slice(c * QCOLS, (c + 1) * QCOLS)
            straight = psum.tile([P, FEAT], F32, tag="raw")
            crossed = psum.tile([P, FEAT], F32, tag="rot")
            for b in range(BATCH):
                mx_pass(straight[:, b * QCOLS : (b + 1) * QCOLS], packed_of[n], b, "straight", cols)
                mx_pass(crossed[:, b * QCOLS : (b + 1) * QCOLS], packed_of[n], b, "crossed", cols)
            banks[c] = [bank[:].rearrange("p (g m f) -> p g m f", m=PER_QUARTER, f=4) for bank in (straight, crossed)]

        def cosine_quarter(n, c):
            if c == 0:
                cos_part[n] = rope.tile([P, LANES // 2, PAIRS, 4], F32, name="turned_by_cos")
                rotated_of[n] = rope.tile([P, LANES // 2, PAIRS, 4], F32, name="rotated")
            straight = banks[c][0]
            if c in VECTOR_QUARTERS:
                nc.vector.tensor_tensor(
                    out=cos_part[n][:, :, c:PAIRS:QUARTERS, :],
                    in0=straight,
                    in1=cos_tab[:, n, c:PAIRS:QUARTERS].unsqueeze(1).unsqueeze(3).to_broadcast(
                        [P, LANES // 2, PER_QUARTER, 4]
                    ),
                    op=ALU.mult,
                )
            else:
                for m in range(PER_QUARTER):
                    j = QUARTERS * m + c
                    nc.scalar.activation(
                        out=cos_part[n][:, :, j, :], in_=straight[:, :, m, :], func=ACT.Copy,
                        scale=cos_tab[:, n, j : j + 1],
                    )

        def sine_quarter(n, c):
            for m in range(PER_QUARTER):
                j = QUARTERS * m + c
                nc.vector.scalar_tensor_tensor(
                    out=rotated_of[n][:, :, j, :], in0=banks[c][1][:, :, m, :],
                    scalar=sin_tab[:, n, j : j + 1], in1=cos_part[n][:, :, j, :],
                    op0=ALU.mult, op1=ALU.add,
                )

        def project_values(n):
            banks["v"] = []
            for b in range(BATCH):
                values = psum.tile([P, FEAT], F32, tag="val")
                mx_pass(values[:], packed_of[n], b, "v", slice(0, FEAT))
                banks["v"].append(values)

        def copy_values(i, b, stage_v):
            nc.scalar.copy(
                out=stage_v[:, b, :, i, :], in_=banks["v"][b][:].rearrange("p (h d) -> p h d", h=HEADS)
            )

        def sort_slot(n, i, stage_qk):
            for l in range(2):
                nc.gpsimd.tensor_scalar(
                    out=stage_qk[:, :, :, i, :].rearrange(
                        "p b (w l h) (j e) -> p (b w) l h j e", w=2, l=2, e=2
                    )[:, :, l],
                    in0=rotated_of[n][:].rearrange("p (a h) j (l e) -> p a h j l e", h=4, l=2)[:, :, :, :, l, :],
                    scalar1=1.0, scalar2=0.0, op0=ALU.mult, op1=ALU.add,
                )

        def store(dst, b, s, src):
            run = RUNS[s]
            nc.sync.dma_start(
                out=dst[b, :, firsts[s] : firsts[s] + P * run, :].rearrange("h (p i) d -> p h (i d)", i=run),
                in_=src.rearrange("p h i d -> p h (i d)"),
            )

        prepare_quarter(0)
        turn_slot(0)
        for b in range(BATCH):
            gain_slot(0, b)
        quantise_slot(0)
        for n in range(SLOTS):
            s, i = slots[n]
            more = n + 1 < SLOTS
            if i == 0:
                stage_qk = stage.tile([P, BATCH, QK, RUNS[s], HEAD_DIM], F32)
                stage_v = stage.tile([P, BATCH, HEADS, RUNS[s], HEAD_DIM], F32)
            for c in range(QUARTERS):
                if n == 0 and c > 0:
                    prepare_quarter(c)
                if n == 0 and c == 2:
                    make_tables(slice(RUNS[0], SLOTS))
                if c == 3:
                    if n == 0:
                        prepare_values()
                    project_values(n)
                project_quarter(n, c)
                if c == 1 and more:
                    turn_slot(n + 1)
                cosine_quarter(n, c)
                sine_quarter(n, c)
                if c == 1 and more:
                    gain_slot(n + 1, 0)
                if c == 2 and more:
                    gain_slot(n + 1, 1)
                    quantise_slot(n + 1)
            for b in range(BATCH):
                copy_values(i, b, stage_v)
            if n == 0:
                square_slot(2)
                square_slot(3)
                finish_slots(2, 2)
            if n + 4 < SLOTS:
                square_slot(n + 4)
                if n % 2 == 1:
                    finish_slots(n + 3, 2)
            sort_slot(n, i, stage_qk)
            if n + 2 < SLOTS:
                norm_slot(n + 2)
            if i == RUNS[s] - 1:
                for b in range(BATCH):
                    store(out_2, b, s, stage_v[:, b])
                    store(out_0, b, s, stage_qk[:, b, 0:HEADS])
                    store(out_1, b, s, stage_qk[:, b, HEADS:QK])
